import numpy as np
import ml_dtypes


def mxq(x, axis, fmt="e4m3"):
    dtype, down = {"e4m3": (ml_dtypes.float8_e4m3fn, 7), "e5m2": (ml_dtypes.float8_e5m2, 14)}[fmt]
    v = np.moveaxis(np.asarray(x, np.float32).astype(ml_dtypes.bfloat16).astype(np.float64), axis, -1)
    blocks = v.reshape(v.shape[:-1] + (-1, 32))
    amax = np.abs(blocks).max(-1, keepdims=True)
    byte = np.maximum(np.where(amax > 0, np.frexp(amax)[1] - 1 + 127, 0) - down, 1)
    scale = np.exp2(byte - 127.0)
    codes = (blocks / scale).astype(np.float32).astype(dtype).astype(np.float64)
    return np.moveaxis((codes * scale).reshape(v.shape), -1, axis)


WIDE = False


def mx_kscale(k):
    if not WIDE:
        return np.ones(k)
    levels = np.array([10, -10, 5, -5, 0])
    if k % 512:
        return np.exp2(np.random.permutation(np.resize(levels, k // 32))).repeat(32)
    a = np.empty((k // 512, 16))
    for p in range(k // 512):
        a[p, :8] = np.random.permutation(np.resize(levels, 8))
        for g in range(8):
            far = levels[np.abs(levels - a[p, g]) >= 10]
            a[p, g + 8] = far[np.random.randint(len(far))]
    return np.exp2(a.ravel()).repeat(32)


BF16 = ml_dtypes.bfloat16


def bf(x):
    return np.asarray(x, np.float32).astype(BF16)


def f64(x):
    return np.asarray(x).astype(np.float64)


B, Q, K, D = 2, 128, 512, 512
NEG = -10000.0


def setup_inputs():
    s, t = mx_kscale(D), mx_kscale(D)
    return {"query": bf(np.random.standard_normal((B, Q, D)) * s),
            "context": bf(np.random.standard_normal((B, K, D)) * 0.5 / t),
            "query_bit": bf(np.random.random((B, Q)) > 0.25),
            "context_bit": bf(np.random.random((B, K)) > 0.25),
            "W_in": bf(np.random.standard_normal((D, D)) * 4.0 / D * t[:, None] / s[None, :]),
            "b_in": bf(np.random.standard_normal(D) / np.sqrt(D) * t)}


def reference(query, context, query_bit, context_bit, W_in, b_in):
    ext = (1.0 - f64(query_bit)[:, :, None] * f64(context_bit)[:, None, :]) * NEG
    q = (mxq(f64(query), 2, "e4m3") @ mxq(f64(W_in), 1, "e4m3").T) + f64(b_in)
    scores = (mxq(q, 2, "e4m3") @ mxq(f64(context), 2, "e4m3").transpose(0, 2, 1)) + ext
    e = np.exp(scores - scores.max(-1, keepdims=True))
    return e / e.sum(-1, keepdims=True)

@@ -1,0 +1,237 @@
+from contextlib import ExitStack
+
+import concourse.mybir as mybir
+from concourse.masks import make_identity
+
+F32 = mybir.dt.float32
+BF16 = mybir.dt.bfloat16
+U32 = mybir.dt.uint32
+U8 = mybir.dt.uint8
+FP8X4 = mybir.dt.float8_e4m3fn_x4
+ALU = mybir.AluOpType
+ACT = mybir.ActivationFunctionType
+
+P = 128
+B = 2
+Q = 128
+K = 512
+D = 512
+PACK = 4
+WARM_PASSES = 8
+WARM_COLS = 256
+NEG = -10000.0
+
+FLOPS = 2 * B * Q * D * D + 2 * B * Q * K * D
+
+
+def tile_attention_pa_s_kernel(tc, query, context, query_bit, context_bit, W_in, b_in, out):
+    nc = tc.nc
+    with ExitStack() as ctx:
+        keep = ctx.enter_context(tc.tile_pool(name="keep", bufs=1))
+        tp = ctx.enter_context(tc.psum_pool(name="tp", bufs=4))
+        spread = ctx.enter_context(tc.psum_pool(name="spread", bufs=1))
+        acc = ctx.enter_context(tc.psum_pool(name="acc", bufs=2))
+        idle = ctx.enter_context(tc.psum_pool(name="idle", bufs=1))
+        ctx.enter_context(tc.manual_schedule())
+
+        query_sb = keep.tile([P, B, D], BF16)
+        w_sb = keep.tile([P, 2, 2, D], BF16)
+        ctx_sb = keep.tile([P, B, 2, 2, D], BF16)
+        cb_col = keep.tile([P, B, 2, 2], BF16)
+        qb_col = keep.tile([P, B], BF16)
+        bias_col = keep.tile([P, PACK], BF16)
+        w_rows = W_in.rearrange("(p u e) d -> u p e d", u=2, e=2)
+        ctx_rows = context.rearrange("b (p g e) d -> b g p e d", g=2, e=2)
+        for b in range(B):
+            nc.sync.dma_start(out=query_sb[:, b, :], in_=query[b])
+        for u in range(2):
+            nc.sync.dma_start(out=w_sb[:, u], in_=w_rows[u])
+        nc.sync.dma_start(out=ctx_sb[:, 0, 0], in_=ctx_rows[0, 0])
+        nc.sync.dma_start(
+            out=bias_col[:].rearrange("p (u e) -> p u e", u=2), in_=b_in.rearrange("(p u e) -> p u e", u=2, e=2)
+        )
+        nc.sync.dma_start(out=ctx_sb[:, 0, 1], in_=ctx_rows[0, 1])
+        nc.sync.dma_start(
+            out=cb_col[:].rearrange("p b g e -> p b (g e)"), in_=context_bit.rearrange("b (p c) -> p b c", c=4)
+        )
+        with nc.allow_non_contiguous_dma(reason="256 single elements, one to a partition and batch"):
+            nc.sync.dma_start(out=qb_col[:], in_=query_bit.rearrange("b i -> i b"))
+        nc.sync.dma_start(out=ctx_sb[:, 1, 0], in_=ctx_rows[1, 0])
+        nc.sync.dma_start(out=ctx_sb[:, 1, 1], in_=ctx_rows[1, 1])
+
+        zeros = keep.tile([P, WARM_COLS * PACK], BF16, align_bytes=64)
+        zero_codes = keep.tile([P, WARM_COLS], U32, align_bytes=64)
+        zero_scales = keep.tile([P, WARM_COLS], U8, align_bytes=64)
+        nc.vector.memset(zeros[:], 0.0)
+        nc.vector.quantize_mx(out=zero_codes[:].bitcast(FP8X4), scales=zero_scales[:], in_=zeros[:])
+        idle_ps = idle.tile([P, WARM_COLS], F32)
+        for n in range(WARM_PASSES):
+            nc.tensor.matmul_mx(
+                out=idle_ps[:],
+                lhsT=zero_codes[:, 0:P].bitcast(FP8X4),
+                lhsT_scale=zero_scales[:, 0:P],
+                rhs=zero_codes[:].bitcast(FP8X4),
+                rhs_scale=zero_scales[:],
+                start=True,
+                stop=True,
+            )
+
+        ident = keep.tile([P, P], F32)
+        make_identity(nc, ident[:])
+        warm = keep.tile([P, 1], F32)
+        nc.vector.memset(warm[:], 0.0)
+        nc.scalar.activation(out=warm[:], in_=warm[:], func=ACT.Exp)
+
+        query_grp = keep.tile([P, B, Q, PACK], BF16, align_bytes=64)
+        query_codes = keep.tile([P, B, Q], U32, align_bytes=64)
+        query_scales = keep.tile([P, B, Q], U8, align_bytes=64)
+        w_grp = keep.tile([P, 2, 2, P, PACK], BF16, align_bytes=64)
+        w_codes = keep.tile([P, 2, 2, P], U32, align_bytes=64)
+        w_scales = keep.tile([P, 2, 2, P], U8, align_bytes=64)
+        ctx_grp = keep.tile([P, B, 2, P, 2, PACK], BF16, align_bytes=64)
+        ctx_codes = keep.tile([P, B, 2, 2 * P], U32, align_bytes=64)
+        ctx_scales = keep.tile([P, B, 2, 2 * P], U8, align_bytes=64)
+        qt_grp = keep.tile([P, B, Q, PACK], BF16, align_bytes=64)
+        qt_codes = keep.tile([P, B, Q], U32, align_bytes=64)
+        qt_scales = keep.tile([P, B, Q], U8, align_bytes=64)
+
+        def transpose_two_row_tiles(words):
+            bank = tp.tile([P, 2, 2, P], F32)
+            for a in range(2):
+                for u in range(2):
+                    nc.tensor.transpose(bank[:, a, u, :], words[:, a, u : 2 * P : 2], ident[:])
+            return bank
+
+        def quantise(grp, codes, scales):
+            nc.vector.quantize_mx(out=codes.bitcast(FP8X4), scales=scales, in_=grp)
+
+        def quantise_query():
+            quantise(
+                query_grp[:].rearrange("p b i t -> p (b i t)"),
+                query_codes[:].rearrange("p b i -> p (b i)"),
+                query_scales[:].rearrange("p b i -> p (b i)"),
+            )
+
+        def quantise_w(u):
+            quantise(
+                w_grp[:, u].rearrange("p e m t -> p (e m t)"),
+                w_codes[:, u].rearrange("p e m -> p (e m)"),
+                w_scales[:, u].rearrange("p e m -> p (e m)"),
+            )
+
+        def quantise_context(b, g):
+            quantise(ctx_grp[:, b, g].rearrange("p r e t -> p (r e t)"), ctx_codes[:, b, g, :], ctx_scales[:, b, g, :])
+
+        def quantise_qt(b):
+            quantise(qt_grp[:, b].rearrange("p i t -> p (i t)"), qt_codes[:, b, :], qt_scales[:, b, :])
+
+        def move_w(u):
+            bank = transpose_two_row_tiles(w_sb[:].bitcast(F32)[:, u])
+            nc.scalar.copy(out=w_grp[:, u].bitcast(F32), in_=bank[:].rearrange("p e u m -> p e m u"))
+
+        def move_context(b, g):
+            bank = transpose_two_row_tiles(ctx_sb[:].bitcast(F32)[:, b, g])
+            nc.scalar.copy(out=ctx_grp[:, b, g].bitcast(F32), in_=bank[:].rearrange("p e u r -> p r e u"))
+
+        def project(b):
+            qt_ps = acc.tile([P, PACK, Q], F32, tag="acc")
+            for u in range(2):
+                for e in range(2):
+                    nc.tensor.matmul_mx(
+                        out=qt_ps[:, 2 * u + e, :],
+                        lhsT=w_codes[:, u, e, :].bitcast(FP8X4),
+                        lhsT_scale=w_scales[:, u, e, :],
+                        rhs=query_codes[:, b, :].bitcast(FP8X4),
+                        rhs_scale=query_scales[:, b, :],
+                        start=True,
+                        stop=True,
+                    )
+            return qt_ps
+
+        def add_bias(b, qt_ps):
+            nc.vector.tensor_tensor(
+                out=qt_grp[:, b],
+                in0=qt_ps[:].rearrange("p t i -> p i t"),
+                in1=bias_col[:].unsqueeze(1).to_broadcast([P, Q, PACK]),
+                op=ALU.add,
+            )
+
+        bank = transpose_two_row_tiles(query_sb[:].bitcast(F32))
+        nc.scalar.copy(out=query_grp[:].bitcast(F32), in_=bank[:].rearrange("p b u i -> p b i u"))
+        move_w(0)
+        quantise_query()
+        move_w(1)
+        quantise_w(0)
+        move_context(0, 0)
+        quantise_w(1)
+        move_context(0, 1)
+        quantise_context(0, 0)
+        qt_ps0 = project(0)
+        qt_ps1 = project(1)
+        quantise_context(0, 1)
+        add_bias(0, qt_ps0)
+        move_context(1, 0)
+        add_bias(1, qt_ps1)
+        quantise_qt(0)
+        move_context(1, 1)
+        quantise_qt(1)
+        quantise_context(1, 0)
+
+        not_cb = keep.tile([P, B, 2, 2], BF16)
+        nc.gpsimd.tensor_scalar(out=not_cb[:], in0=cb_col[:], scalar1=-1.0, scalar2=1.0, op0=ALU.mult, op1=ALU.add)
+        neg_qb = keep.tile([P, B], F32)
+        nc.gpsimd.tensor_scalar(out=neg_qb[:], in0=qb_col[:], scalar1=NEG, scalar2=0.0, op0=ALU.mult, op1=ALU.add)
+        spread_ps = spread.tile([P, B, 2, P], F32)
+        for b in range(B):
+            for g in range(2):
+                nc.tensor.transpose(spread_ps[:, b, g, :], not_cb[:].bitcast(F32)[:, b, g, :].to_broadcast([P, P]), ident[:])
+        not_cb_all = keep.tile([P, B, K], BF16)
+        nc.scalar.copy(out=not_cb_all[:].bitcast(F32), in_=spread_ps[:].rearrange("p b g n -> p b (g n)"))
+        quantise_context(1, 1)
+
+        masked = keep.tile([P, B, K], F32)
+        expd = keep.tile([P, B, K], F32)
+        prob = keep.tile([P, B, K], F32)
+        neg_max = keep.tile([P, B], F32)
+        row_sum = keep.tile([P, B], F32)
+        inv_sum = keep.tile([P, B], F32)
+        for b in range(B):
+            score_ps = acc.tile([P, K], F32, tag="acc")
+            nc.tensor.matmul_mx(
+                out=score_ps[:],
+                lhsT=qt_codes[:, b, :].bitcast(FP8X4),
+                lhsT_scale=qt_scales[:, b, :],
+                rhs=ctx_codes[:, b].rearrange("p g n -> p (g n)").bitcast(FP8X4),
+                rhs_scale=ctx_scales[:, b].rearrange("p g n -> p (g n)"),
+                start=True,
+                stop=True,
+            )
+            nc.vector.scalar_tensor_tensor(
+                out=masked[:, b, :],
+                in0=not_cb_all[:, b, :],
+                scalar=neg_qb[:, b : b + 1],
+                in1=score_ps[:],
+                op0=ALU.mult,
+                op1=ALU.add,
+            )
+            nc.vector.tensor_reduce(
+                out=neg_max[:, b : b + 1], in_=masked[:, b, :], axis=mybir.AxisListType.X, op=ALU.max, negate=True
+            )
+            nc.scalar.activation(
+                out=expd[:, b, :],
+                in_=masked[:, b, :],
+                func=ACT.Exp,
+                bias=neg_max[:, b : b + 1],
+                scale=1.0,
+                accum_out=row_sum[:, b : b + 1],
+            )
+        for b in range(B):
+            nc.vector.reciprocal(inv_sum[:, b : b + 1], row_sum[:, b : b + 1])
+            nc.vector.tensor_scalar(
+                out=prob[:, b, :].rearrange("i (p g e) -> i p g e", g=2, e=2),
+                in0=expd[:, b, :].rearrange("i (g p e) -> i p g e", g=2, e=2),
+                scalar1=inv_sum[:, b : b + 1],
+                scalar2=None,
+                op0=ALU.mult,
+            )
+            nc.sync.dma_start(out=out[b], in_=prob[:, b, :])

@@ -41,7 +41,7 @@ def tile_attention_pa_s_kernel(tc, query, context, query_bit, context_bit, W_in,
         qb_col = keep.tile([P, B], BF16)
         bias_col = keep.tile([P, PACK], BF16)
         w_rows = W_in.rearrange("(p u e) d -> u p e d", u=2, e=2)
-        ctx_rows = context.rearrange("b (p g e) d -> b g p e d", g=2, e=2)
+        ctx_rows = context.rearrange("b (g p e) d -> b g p e d", g=2, e=2)
         for b in range(B):
             nc.sync.dma_start(out=query_sb[:, b, :], in_=query[b])
         for u in range(2):
@@ -52,7 +52,7 @@ def tile_attention_pa_s_kernel(tc, query, context, query_bit, context_bit, W_in,
         )
         nc.sync.dma_start(out=ctx_sb[:, 0, 1], in_=ctx_rows[0, 1])
         nc.sync.dma_start(
-            out=cb_col[:].rearrange("p b g e -> p b (g e)"), in_=context_bit.rearrange("b (p c) -> p b c", c=4)
+            out=cb_col[:].rearrange("p b g e -> p (b g) e"), in_=context_bit.rearrange("b (g p e) -> p (b g) e", g=2, e=2)
         )
         with nc.allow_non_contiguous_dma(reason="256 single elements, one to a partition and batch"):
             nc.sync.dma_start(out=qb_col[:], in_=query_bit.rearrange("b i -> i b"))
@@ -228,8 +228,8 @@ def tile_attention_pa_s_kernel(tc, query, context, query_bit, context_bit, W_in,
         for b in range(B):
             nc.vector.reciprocal(inv_sum[:, b : b + 1], row_sum[:, b : b + 1])
             nc.vector.tensor_scalar(
-                out=prob[:, b, :].rearrange("i (p g e) -> i p g e", g=2, e=2),
-                in0=expd[:, b, :].rearrange("i (g p e) -> i p g e", g=2, e=2),
+                out=prob[:, b, :],
+                in0=expd[:, b, :],
                 scalar1=inv_sum[:, b : b + 1],
                 scalar2=None,
                 op0=ALU.mult,

@@ -52,7 +52,7 @@ def tile_attention_pa_s_kernel(tc, query, context, query_bit, context_bit, W_in,
         )
         nc.sync.dma_start(out=ctx_sb[:, 0, 1], in_=ctx_rows[0, 1])
         nc.sync.dma_start(
-            out=cb_col[:].rearrange("p b g e -> p (b g) e"), in_=context_bit.rearrange("b (g p e) -> p (b g) e", g=2, e=2)
+            out=cb_col[:].rearrange("p b g e -> p b (g e)"), in_=context_bit.rearrange("b (p c) -> p b c", c=4)
         )
         with nc.allow_non_contiguous_dma(reason="256 single elements, one to a partition and batch"):
             nc.sync.dma_start(out=qb_col[:], in_=query_bit.rearrange("b i -> i b"))
@@ -186,7 +186,9 @@ def tile_attention_pa_s_kernel(tc, query, context, query_bit, context_bit, W_in,
             for g in range(2):
                 nc.tensor.transpose(spread_ps[:, b, g, :], not_cb[:].bitcast(F32)[:, b, g, :].to_broadcast([P, P]), ident[:])
         not_cb_all = keep.tile([P, B, K], BF16)
-        nc.scalar.copy(out=not_cb_all[:].bitcast(F32), in_=spread_ps[:].rearrange("p b g n -> p b (g n)"))
+        nc.scalar.copy(
+            out=not_cb_all[:].bitcast(F32).rearrange("p b (n g) -> p b n g", g=2), in_=spread_ps[:].rearrange("p b g n -> p b n g")
+        )
         quantise_context(1, 1)
 
         masked = keep.tile([P, B, K], F32)

@@ -18,7 +18,6 @@ K = 512
 D = 512
 PACK = 4
 WARM_PASSES = 8
-WARM_COLS = 256
 NEG = -10000.0
 
 FLOPS = 2 * B * Q * D * D + 2 * B * Q * K * D
@@ -30,8 +29,7 @@ def tile_attention_pa_s_kernel(tc, query, context, query_bit, context_bit, W_in,
         keep = ctx.enter_context(tc.tile_pool(name="keep", bufs=1))
         tp = ctx.enter_context(tc.psum_pool(name="tp", bufs=4))
         spread = ctx.enter_context(tc.psum_pool(name="spread", bufs=1))
-        acc = ctx.enter_context(tc.psum_pool(name="acc", bufs=2))
-        idle = ctx.enter_context(tc.psum_pool(name="idle", bufs=1))
+        acc = ctx.enter_context(tc.psum_pool(name="acc", bufs=3))
         ctx.enter_context(tc.manual_schedule())
 
         query_sb = keep.tile([P, B, D], BF16)
@@ -59,17 +57,17 @@ def tile_attention_pa_s_kernel(tc, query, context, query_bit, context_bit, W_in,
         nc.sync.dma_start(out=ctx_sb[:, 1, 0], in_=ctx_rows[1, 0])
         nc.sync.dma_start(out=ctx_sb[:, 1, 1], in_=ctx_rows[1, 1])
 
-        zeros = keep.tile([P, WARM_COLS * PACK], BF16, align_bytes=64)
-        zero_codes = keep.tile([P, WARM_COLS], U32, align_bytes=64)
-        zero_scales = keep.tile([P, WARM_COLS], U8, align_bytes=64)
-        nc.vector.memset(zeros[:], 0.0)
+        zeros = keep.tile([P, P * PACK], BF16, align_bytes=64)
+        zero_codes = keep.tile([P, P], U32, align_bytes=64)
+        zero_scales = keep.tile([P, P], U8, align_bytes=64)
+        nc.gpsimd.memset(zeros[:], 0.0)
         nc.vector.quantize_mx(out=zero_codes[:].bitcast(FP8X4), scales=zero_scales[:], in_=zeros[:])
-        idle_ps = idle.tile([P, WARM_COLS], F32)
+        idle_ps = acc.tile([P, P], F32, tag="acc")
         for n in range(WARM_PASSES):
             nc.tensor.matmul_mx(
                 out=idle_ps[:],
-                lhsT=zero_codes[:, 0:P].bitcast(FP8X4),
-                lhsT_scale=zero_scales[:, 0:P],
+                lhsT=zero_codes[:].bitcast(FP8X4),
+                lhsT_scale=zero_scales[:],
                 rhs=zero_codes[:].bitcast(FP8X4),
                 rhs_scale=zero_scales[:],
                 start=True,
@@ -168,14 +166,14 @@ def tile_attention_pa_s_kernel(tc, query, context, query_bit, context_bit, W_in,
         quantise_context(0, 0)
         qt_ps0 = project(0)
         qt_ps1 = project(1)
-        quantise_context(0, 1)
         add_bias(0, qt_ps0)
         move_context(1, 0)
-        add_bias(1, qt_ps1)
+        quantise_context(0, 1)
         quantise_qt(0)
         move_context(1, 1)
-        quantise_qt(1)
+        add_bias(1, qt_ps1)
         quantise_context(1, 0)
+        quantise_qt(1)
 
         not_cb = keep.tile([P, B, 2, 2], BF16)
         nc.gpsimd.tensor_scalar(out=not_cb[:], in0=cb_col[:], scalar1=-1.0, scalar2=1.0, op0=ALU.mult, op1=ALU.add)
@@ -189,7 +187,6 @@ def tile_attention_pa_s_kernel(tc, query, context, query_bit, context_bit, W_in,
         nc.scalar.copy(
             out=not_cb_all[:].bitcast(F32).rearrange("p b (n g) -> p b n g", g=2), in_=spread_ps[:].rearrange("p b g n -> p b n g")
         )
-        quantise_context(1, 1)
 
         masked = keep.tile([P, B, K], F32)
         expd = keep.tile([P, B, K], F32)
@@ -197,28 +194,36 @@ def tile_attention_pa_s_kernel(tc, query, context, query_bit, context_bit, W_in,
         neg_max = keep.tile([P, B], F32)
         row_sum = keep.tile([P, B], F32)
         inv_sum = keep.tile([P, B], F32)
-        for b in range(B):
-            score_ps = acc.tile([P, K], F32, tag="acc")
+        def score(b, g0, g1):
+            score_ps = acc.tile([P, (g1 - g0) * 2 * P], F32, tag="acc")
             nc.tensor.matmul_mx(
                 out=score_ps[:],
                 lhsT=qt_codes[:, b, :].bitcast(FP8X4),
                 lhsT_scale=qt_scales[:, b, :],
-                rhs=ctx_codes[:, b].rearrange("p g n -> p (g n)").bitcast(FP8X4),
-                rhs_scale=ctx_scales[:, b].rearrange("p g n -> p (g n)"),
+                rhs=ctx_codes[:, b, g0:g1].rearrange("p g n -> p (g n)").bitcast(FP8X4),
+                rhs_scale=ctx_scales[:, b, g0:g1].rearrange("p g n -> p (g n)"),
                 start=True,
                 stop=True,
             )
+            return score_ps
+
+        def add_mask(b, g0, g1, score_ps):
+            cols = slice(g0 * 2 * P, g1 * 2 * P)
             nc.vector.scalar_tensor_tensor(
-                out=masked[:, b, :],
-                in0=not_cb_all[:, b, :],
+                out=masked[:, b, cols],
+                in0=not_cb_all[:, b, cols],
                 scalar=neg_qb[:, b : b + 1],
                 in1=score_ps[:],
                 op0=ALU.mult,
                 op1=ALU.add,
             )
+
+        def row_max(b):
             nc.vector.tensor_reduce(
                 out=neg_max[:, b : b + 1], in_=masked[:, b, :], axis=mybir.AxisListType.X, op=ALU.max, negate=True
             )
+
+        def exponential(b):
             nc.scalar.activation(
                 out=expd[:, b, :],
                 in_=masked[:, b, :],
@@ -227,6 +232,18 @@ def tile_attention_pa_s_kernel(tc, query, context, query_bit, context_bit, W_in,
                 scale=1.0,
                 accum_out=row_sum[:, b : b + 1],
             )
+
+        score_0 = score(0, 0, 2)
+        score_1a = score(1, 0, 1)
+        quantise_context(1, 1)
+        score_1b = score(1, 1, 2)
+        add_mask(0, 0, 2, score_0)
+        add_mask(1, 0, 1, score_1a)
+        add_mask(1, 1, 2, score_1b)
+        row_max(0)
+        row_max(1)
+        exponential(0)
+        exponential(1)
         for b in range(B):
             nc.vector.reciprocal(inv_sum[:, b : b + 1], row_sum[:, b : b + 1])
             nc.vector.tensor_scalar(

@@ -40,10 +40,10 @@ def tile_attention_pa_s_kernel(tc, query, context, query_bit, context_bit, W_in,
         bias_col = keep.tile([P, PACK], BF16)
         w_rows = W_in.rearrange("(p u e) d -> u p e d", u=2, e=2)
         ctx_rows = context.rearrange("b (g p e) d -> b g p e d", g=2, e=2)
-        for b in range(B):
-            nc.sync.dma_start(out=query_sb[:, b, :], in_=query[b])
+        nc.sync.dma_start(out=query_sb[:, 0, :], in_=query[0])
         for u in range(2):
             nc.sync.dma_start(out=w_sb[:, u], in_=w_rows[u])
+        nc.sync.dma_start(out=query_sb[:, 1, :], in_=query[1])
         nc.sync.dma_start(out=ctx_sb[:, 0, 0], in_=ctx_rows[0, 0])
         nc.sync.dma_start(
             out=bias_col[:].rearrange("p (u e) -> p u e", u=2), in_=b_in.rearrange("(p u e) -> p u e", u=2, e=2)
@@ -103,12 +103,14 @@ def tile_attention_pa_s_kernel(tc, query, context, query_bit, context_bit, W_in,
         def quantise(grp, codes, scales):
             nc.vector.quantize_mx(out=codes.bitcast(FP8X4), scales=scales, in_=grp)
 
-        def quantise_query():
-            quantise(
-                query_grp[:].rearrange("p b i t -> p (b i t)"),
-                query_codes[:].rearrange("p b i -> p (b i)"),
-                query_scales[:].rearrange("p b i -> p (b i)"),
-            )
+        def quantise_query(b):
+            quantise(query_grp[:, b].rearrange("p i t -> p (i t)"), query_codes[:, b, :], query_scales[:, b, :])
+
+        def move_query(b):
+            bank = tp.tile([P, 2, P], F32)
+            for u in range(2):
+                nc.tensor.transpose(bank[:, u, :], query_sb[:].bitcast(F32)[:, b, u : 2 * P : 2], ident[:])
+            nc.vector.tensor_copy(out=query_grp[:, b].bitcast(F32), in_=bank[:].rearrange("p u i -> p i u"))
 
         def quantise_w(u):
             quantise(
@@ -154,14 +156,15 @@ def tile_attention_pa_s_kernel(tc, query, context, query_bit, context_bit, W_in,
                 op=ALU.add,
             )
 
-        bank = transpose_two_row_tiles(query_sb[:].bitcast(F32))
-        nc.scalar.copy(out=query_grp[:].bitcast(F32), in_=bank[:].rearrange("p b u i -> p b i u"))
+        move_query(0)
         move_w(0)
-        quantise_query()
+        quantise_query(0)
         move_w(1)
         quantise_w(0)
-        move_context(0, 0)
+        move_query(1)
         quantise_w(1)
+        move_context(0, 0)
+        quantise_query(1)
         move_context(0, 1)
         quantise_context(0, 0)
         qt_ps0 = project(0)
@@ -233,12 +236,18 @@ def tile_attention_pa_s_kernel(tc, query, context, query_bit, context_bit, W_in,
                 accum_out=row_sum[:, b : b + 1],
             )
 
+        mask_1a = keep.tile([P, 2 * P], F32)
+        score_1a_sb = keep.tile([P, 2 * P], F32)
+        nc.gpsimd.tensor_scalar(
+            out=mask_1a[:], in0=not_cb_all[:, 1, 0 : 2 * P], scalar1=neg_qb[:, 1:2], scalar2=0.0, op0=ALU.mult, op1=ALU.add
+        )
         score_0 = score(0, 0, 2)
         score_1a = score(1, 0, 1)
+        nc.scalar.copy(out=score_1a_sb[:], in_=score_1a[:])
+        nc.gpsimd.tensor_tensor(out=masked[:, 1, 0 : 2 * P], in0=score_1a_sb[:], in1=mask_1a[:], op=ALU.add)
         quantise_context(1, 1)
         score_1b = score(1, 1, 2)
         add_mask(0, 0, 2, score_0)
-        add_mask(1, 0, 1, score_1a)
         add_mask(1, 1, 2, score_1b)
         row_max(0)
         row_max(1)

@@ -49,13 +49,13 @@ def tile_attention_pa_s_kernel(tc, query, context, query_bit, context_bit, W_in,
             out=bias_col[:].rearrange("p (u e) -> p u e", u=2), in_=b_in.rearrange("(p u e) -> p u e", u=2, e=2)
         )
         nc.sync.dma_start(out=ctx_sb[:, 0, 1], in_=ctx_rows[0, 1])
+        nc.sync.dma_start(out=ctx_sb[:, 1, 0], in_=ctx_rows[1, 0])
+        nc.sync.dma_start(out=ctx_sb[:, 1, 1], in_=ctx_rows[1, 1])
         nc.sync.dma_start(
             out=cb_col[:].rearrange("p b g e -> p b (g e)"), in_=context_bit.rearrange("b (p c) -> p b c", c=4)
         )
         with nc.allow_non_contiguous_dma(reason="256 single elements, one to a partition and batch"):
             nc.sync.dma_start(out=qb_col[:], in_=query_bit.rearrange("b i -> i b"))
-        nc.sync.dma_start(out=ctx_sb[:, 1, 0], in_=ctx_rows[1, 0])
-        nc.sync.dma_start(out=ctx_sb[:, 1, 1], in_=ctx_rows[1, 1])
 
         zeros = keep.tile([P, P * PACK], BF16, align_bytes=64)
         zero_codes = keep.tile([P, P], U32, align_bytes=64)

@@ -17,7 +17,6 @@ Q = 128
 K = 512
 D = 512
 PACK = 4
-WARM_PASSES = 8
 NEG = -10000.0
 
 FLOPS = 2 * B * Q * D * D + 2 * B * Q * K * D
@@ -56,23 +55,6 @@ def tile_attention_pa_s_kernel(tc, query, context, query_bit, context_bit, W_in,
         )
         with nc.allow_non_contiguous_dma(reason="256 single elements, one to a partition and batch"):
             nc.sync.dma_start(out=qb_col[:], in_=query_bit.rearrange("b i -> i b"))
-
-        zeros = keep.tile([P, P * PACK], BF16, align_bytes=64)
-        zero_codes = keep.tile([P, P], U32, align_bytes=64)
-        zero_scales = keep.tile([P, P], U8, align_bytes=64)
-        nc.gpsimd.memset(zeros[:], 0.0)
-        nc.vector.quantize_mx(out=zero_codes[:].bitcast(FP8X4), scales=zero_scales[:], in_=zeros[:])
-        idle_ps = acc.tile([P, P], F32, tag="acc")
-        for n in range(WARM_PASSES):
-            nc.tensor.matmul_mx(
-                out=idle_ps[:],
-                lhsT=zero_codes[:].bitcast(FP8X4),
-                lhsT_scale=zero_scales[:],
-                rhs=zero_codes[:].bitcast(FP8X4),
-                rhs_scale=zero_scales[:],
-                start=True,
-                stop=True,
-            )
 
         ident = keep.tile([P, P], F32)
         make_identity(nc, ident[:])

@@ -235,13 +235,18 @@ def tile_attention_pa_s_kernel(tc, query, context, query_bit, context_bit, W_in,
         row_max(1)
         exponential(0)
         exponential(1)
-        for b in range(B):
-            nc.vector.reciprocal(inv_sum[:, b : b + 1], row_sum[:, b : b + 1])
+        def normalise_and_store(b, c0, c1):
             nc.vector.tensor_scalar(
-                out=prob[:, b, :],
-                in0=expd[:, b, :],
+                out=prob[:, b, c0:c1],
+                in0=expd[:, b, c0:c1],
                 scalar1=inv_sum[:, b : b + 1],
                 scalar2=None,
                 op0=ALU.mult,
             )
-            nc.sync.dma_start(out=out[b], in_=prob[:, b, :])
+            nc.sync.dma_start(out=out[b][:, c0:c1], in_=prob[:, b, c0:c1])
+
+        nc.vector.reciprocal(inv_sum[:, 0:1], row_sum[:, 0:1])
+        normalise_and_store(0, 0, K)
+        nc.vector.reciprocal(inv_sum[:, 1:2], row_sum[:, 1:2])
+        normalise_and_store(1, 0, K // 2)
+        normalise_and_store(1, K // 2, K)

@@ -26,35 +26,33 @@ def tile_attention_pa_s_kernel(tc, query, context, query_bit, context_bit, W_in,
     nc = tc.nc
     with ExitStack() as ctx:
         keep = ctx.enter_context(tc.tile_pool(name="keep", bufs=1))
-        tp = ctx.enter_context(tc.psum_pool(name="tp", bufs=4))
-        spread = ctx.enter_context(tc.psum_pool(name="spread", bufs=1))
-        acc = ctx.enter_context(tc.psum_pool(name="acc", bufs=3))
+        psum = ctx.enter_context(tc.psum_pool(name="psum", bufs=8))
         ctx.enter_context(tc.manual_schedule())
 
         query_sb = keep.tile([P, B, D], BF16)
         w_sb = keep.tile([P, 2, 2, D], BF16)
         ctx_sb = keep.tile([P, B, 2, 2, D], BF16)
-        cb_col = keep.tile([P, B, 2, 2], BF16)
+        cb_col = keep.tile([P, PACK, 2], BF16)
         qb_col = keep.tile([P, B], BF16)
         bias_col = keep.tile([P, PACK], BF16)
         w_rows = W_in.rearrange("(p u e) d -> u p e d", u=2, e=2)
         ctx_rows = context.rearrange("b (g p e) d -> b g p e d", g=2, e=2)
         nc.sync.dma_start(out=query_sb[:, 0, :], in_=query[0])
+        nc.sync.dma_start(
+            out=cb_col[:].rearrange("p c e -> p (c e)"), in_=context_bit.rearrange("b (n c) -> (b n) c", c=2 * PACK)
+        )
         for u in range(2):
             nc.sync.dma_start(out=w_sb[:, u], in_=w_rows[u])
         nc.sync.dma_start(out=query_sb[:, 1, :], in_=query[1])
-        nc.sync.dma_start(out=ctx_sb[:, 0, 0], in_=ctx_rows[0, 0])
+        for g in range(2):
+            nc.sync.dma_start(out=ctx_sb[:, 0, g], in_=ctx_rows[0, g])
         nc.sync.dma_start(
             out=bias_col[:].rearrange("p (u e) -> p u e", u=2), in_=b_in.rearrange("(p u e) -> p u e", u=2, e=2)
         )
-        nc.sync.dma_start(out=ctx_sb[:, 0, 1], in_=ctx_rows[0, 1])
-        nc.sync.dma_start(out=ctx_sb[:, 1, 0], in_=ctx_rows[1, 0])
-        nc.sync.dma_start(out=ctx_sb[:, 1, 1], in_=ctx_rows[1, 1])
-        nc.sync.dma_start(
-            out=cb_col[:].rearrange("p b g e -> p b (g e)"), in_=context_bit.rearrange("b (p c) -> p b c", c=4)
-        )
         with nc.allow_non_contiguous_dma(reason="256 single elements, one to a partition and batch"):
             nc.sync.dma_start(out=qb_col[:], in_=query_bit.rearrange("b i -> i b"))
+        for g in range(2):
+            nc.sync.dma_start(out=ctx_sb[:, 1, g], in_=ctx_rows[1, g])
 
         ident = keep.tile([P, P], F32)
         make_identity(nc, ident[:])
@@ -68,7 +66,8 @@ def tile_attention_pa_s_kernel(tc, query, context, query_bit, context_bit, W_in,
         w_grp = keep.tile([P, 2, 2, P, PACK], BF16, align_bytes=64)
         w_codes = keep.tile([P, 2, 2, P], U32, align_bytes=64)
         w_scales = keep.tile([P, 2, 2, P], U8, align_bytes=64)
-        ctx_grp = keep.tile([P, B, 2, P, 2, PACK], BF16, align_bytes=64)
+        ctx0_grp = keep.tile([P, 2, P, 2, PACK], BF16, align_bytes=64)
+        ctx1_grp = keep.tile([P, 2, 2, P, PACK], BF16, align_bytes=64)
         ctx_codes = keep.tile([P, B, 2, 2 * P], U32, align_bytes=64)
         ctx_scales = keep.tile([P, B, 2, 2 * P], U8, align_bytes=64)
         qt_grp = keep.tile([P, B, Q, PACK], BF16, align_bytes=64)
@@ -76,7 +75,7 @@ def tile_attention_pa_s_kernel(tc, query, context, query_bit, context_bit, W_in,
         qt_scales = keep.tile([P, B, Q], U8, align_bytes=64)
 
         def transpose_two_row_tiles(words):
-            bank = tp.tile([P, 2, 2, P], F32)
+            bank = psum.tile([P, 2, 2, P], F32, tag="bank")
             for a in range(2):
                 for u in range(2):
                     nc.tensor.transpose(bank[:, a, u, :], words[:, a, u : 2 * P : 2], ident[:])
@@ -89,7 +88,7 @@ def tile_attention_pa_s_kernel(tc, query, context, query_bit, context_bit, W_in,
             quantise(query_grp[:, b].rearrange("p i t -> p (i t)"), query_codes[:, b, :], query_scales[:, b, :])
 
         def move_query(b):
-            bank = tp.tile([P, 2, P], F32)
+            bank = psum.tile([P, 2, P], F32, tag="bank")
             for u in range(2):
                 nc.tensor.transpose(bank[:, u, :], query_sb[:].bitcast(F32)[:, b, u : 2 * P : 2], ident[:])
             nc.vector.tensor_copy(out=query_grp[:, b].bitcast(F32), in_=bank[:].rearrange("p u i -> p i u"))
@@ -101,8 +100,14 @@ def tile_attention_pa_s_kernel(tc, query, context, query_bit, context_bit, W_in,
                 w_scales[:, u].rearrange("p e m -> p (e m)"),
             )
 
-        def quantise_context(b, g):
-            quantise(ctx_grp[:, b, g].rearrange("p r e t -> p (r e t)"), ctx_codes[:, b, g, :], ctx_scales[:, b, g, :])
+        def quantise_context_0(g):
+            quantise(ctx0_grp[:, g].rearrange("p r e t -> p (r e t)"), ctx_codes[:, 0, g, :], ctx_scales[:, 0, g, :])
+
+        def quantise_context_1(g, e0, e1):
+            cols = slice(e0 * P, e1 * P)
+            quantise(
+                ctx1_grp[:, g, e0:e1].rearrange("p e r t -> p (e r t)"), ctx_codes[:, 1, g, cols], ctx_scales[:, 1, g, cols]
+            )
 
         def quantise_qt(b):
             quantise(qt_grp[:, b].rearrange("p i t -> p (i t)"), qt_codes[:, b, :], qt_scales[:, b, :])
@@ -111,12 +116,19 @@ def tile_attention_pa_s_kernel(tc, query, context, query_bit, context_bit, W_in,
             bank = transpose_two_row_tiles(w_sb[:].bitcast(F32)[:, u])
             nc.scalar.copy(out=w_grp[:, u].bitcast(F32), in_=bank[:].rearrange("p e u m -> p e m u"))
 
-        def move_context(b, g):
-            bank = transpose_two_row_tiles(ctx_sb[:].bitcast(F32)[:, b, g])
-            nc.scalar.copy(out=ctx_grp[:, b, g].bitcast(F32), in_=bank[:].rearrange("p e u r -> p r e u"))
+        def move_context_0(g):
+            bank = transpose_two_row_tiles(ctx_sb[:].bitcast(F32)[:, 0, g])
+            nc.scalar.copy(out=ctx0_grp[:, g].bitcast(F32), in_=bank[:].rearrange("p e u r -> p r e u"))
+
+        def move_context_1(g):
+            for e in range(2):
+                bank = psum.tile([P, 2, P], F32, tag="bank")
+                for u in range(2):
+                    nc.tensor.transpose(bank[:, u, :], ctx_sb[:].bitcast(F32)[:, 1, g, e, u : 2 * P : 2], ident[:])
+                nc.scalar.copy(out=ctx1_grp[:, g, e].bitcast(F32), in_=bank[:].rearrange("p u r -> p r u"))
 
         def project(b):
-            qt_ps = acc.tile([P, PACK, Q], F32, tag="acc")
+            qt_ps = psum.tile([P, PACK, Q], F32, tag="bank")
             for u in range(2):
                 for e in range(2):
                     nc.tensor.matmul_mx(
@@ -138,40 +150,42 @@ def tile_attention_pa_s_kernel(tc, query, context, query_bit, context_bit, W_in,
                 op=ALU.add,
             )
 
+        not_cb = keep.tile([P, PACK, 2], BF16)
+        nc.vector.tensor_scalar(out=not_cb[:], in0=cb_col[:], scalar1=-1.0, scalar2=1.0, op0=ALU.mult, op1=ALU.add)
         move_query(0)
+        spread_ps = psum.tile([P, PACK, P], F32, tag="bank")
+        for c in range(PACK):
+            nc.tensor.transpose(spread_ps[:, c, :], not_cb[:].bitcast(F32)[:, c, :].to_broadcast([P, P]), ident[:])
         move_w(0)
         quantise_query(0)
         move_w(1)
         quantise_w(0)
         move_query(1)
         quantise_w(1)
-        move_context(0, 0)
+        move_context_0(0)
         quantise_query(1)
-        move_context(0, 1)
-        quantise_context(0, 0)
+        move_context_0(1)
+        quantise_context_0(0)
         qt_ps0 = project(0)
         qt_ps1 = project(1)
         add_bias(0, qt_ps0)
-        move_context(1, 0)
-        quantise_context(0, 1)
-        quantise_qt(0)
-        move_context(1, 1)
-        add_bias(1, qt_ps1)
-        quantise_context(1, 0)
-        quantise_qt(1)
-
-        not_cb = keep.tile([P, B, 2, 2], BF16)
-        nc.gpsimd.tensor_scalar(out=not_cb[:], in0=cb_col[:], scalar1=-1.0, scalar2=1.0, op0=ALU.mult, op1=ALU.add)
-        neg_qb = keep.tile([P, B], F32)
-        nc.gpsimd.tensor_scalar(out=neg_qb[:], in0=qb_col[:], scalar1=NEG, scalar2=0.0, op0=ALU.mult, op1=ALU.add)
-        spread_ps = spread.tile([P, B, 2, P], F32)
-        for b in range(B):
-            for g in range(2):
-                nc.tensor.transpose(spread_ps[:, b, g, :], not_cb[:].bitcast(F32)[:, b, g, :].to_broadcast([P, P]), ident[:])
         not_cb_all = keep.tile([P, B, K], BF16)
         nc.scalar.copy(
-            out=not_cb_all[:].bitcast(F32).rearrange("p b (n g) -> p b n g", g=2), in_=spread_ps[:].rearrange("p b g n -> p b n g")
+            out=not_cb_all[:].bitcast(F32).rearrange("p b (n c) -> p b n c", c=PACK),
+            in_=spread_ps[:].rearrange("p c (b n) -> p b n c", b=B),
         )
+        neg_qb = keep.tile([P, B], F32)
+        nc.gpsimd.tensor_scalar(out=neg_qb[:], in0=qb_col[:], scalar1=NEG, scalar2=0.0, op0=ALU.mult, op1=ALU.add)
+        not_cb_1 = not_cb_all[:, 1].rearrange("p (g r e) -> p g e r", g=2, e=2)
+        mask_1a = keep.tile([P, 2, P], F32)
+        nc.scalar.activation(out=mask_1a[:], in_=not_cb_1[:, 0], func=ACT.Copy, scale=neg_qb[:, 1:2])
+        move_context_1(0)
+        add_bias(1, qt_ps1)
+        move_context_1(1)
+        quantise_qt(0)
+        quantise_context_0(1)
+        quantise_qt(1)
+        quantise_context_1(0, 0, 2)
 
         masked = keep.tile([P, B, K], F32)
         expd = keep.tile([P, B, K], F32)
@@ -179,24 +193,23 @@ def tile_attention_pa_s_kernel(tc, query, context, query_bit, context_bit, W_in,
         neg_max = keep.tile([P, B], F32)
         row_sum = keep.tile([P, B], F32)
         inv_sum = keep.tile([P, B], F32)
-        def score(b, g0, g1):
-            score_ps = acc.tile([P, (g1 - g0) * 2 * P], F32, tag="acc")
+        def score(b, c0, c1):
+            score_ps = psum.tile([P, c1 - c0], F32, tag="bank")
             nc.tensor.matmul_mx(
                 out=score_ps[:],
                 lhsT=qt_codes[:, b, :].bitcast(FP8X4),
                 lhsT_scale=qt_scales[:, b, :],
-                rhs=ctx_codes[:, b, g0:g1].rearrange("p g n -> p (g n)").bitcast(FP8X4),
-                rhs_scale=ctx_scales[:, b, g0:g1].rearrange("p g n -> p (g n)"),
+                rhs=ctx_codes[:, b].rearrange("p g n -> p (g n)")[:, c0:c1].bitcast(FP8X4),
+                rhs_scale=ctx_scales[:, b].rearrange("p g n -> p (g n)")[:, c0:c1],
                 start=True,
                 stop=True,
             )
             return score_ps
 
-        def add_mask(b, g0, g1, score_ps):
-            cols = slice(g0 * 2 * P, g1 * 2 * P)
+        def add_mask(b, c0, c1, mask_bits, score_ps):
             nc.vector.scalar_tensor_tensor(
-                out=masked[:, b, cols],
-                in0=not_cb_all[:, b, cols],
+                out=masked[:, b, c0:c1],
+                in0=mask_bits,
                 scalar=neg_qb[:, b : b + 1],
                 in1=score_ps[:],
                 op0=ALU.mult,
@@ -218,35 +231,37 @@ def tile_attention_pa_s_kernel(tc, query, context, query_bit, context_bit, W_in,
                 accum_out=row_sum[:, b : b + 1],
             )
 
-        mask_1a = keep.tile([P, 2 * P], F32)
         score_1a_sb = keep.tile([P, 2 * P], F32)
-        nc.gpsimd.tensor_scalar(
-            out=mask_1a[:], in0=not_cb_all[:, 1, 0 : 2 * P], scalar1=neg_qb[:, 1:2], scalar2=0.0, op0=ALU.mult, op1=ALU.add
-        )
-        score_0 = score(0, 0, 2)
-        score_1a = score(1, 0, 1)
+        score_0 = score(0, 0, K)
+        score_1a = score(1, 0, 2 * P)
         nc.scalar.copy(out=score_1a_sb[:], in_=score_1a[:])
-        nc.gpsimd.tensor_tensor(out=masked[:, 1, 0 : 2 * P], in0=score_1a_sb[:], in1=mask_1a[:], op=ALU.add)
-        quantise_context(1, 1)
-        score_1b = score(1, 1, 2)
-        add_mask(0, 0, 2, score_0)
-        add_mask(1, 1, 2, score_1b)
+        nc.gpsimd.tensor_tensor(
+            out=masked[:, 1, 0 : 2 * P], in0=score_1a_sb[:], in1=mask_1a[:].rearrange("p e r -> p (e r)"), op=ALU.add
+        )
+        quantise_context_1(1, 0, 1)
+        quantise_context_1(1, 1, 2)
+        score_1b = score(1, 2 * P, 3 * P)
+        score_1c = score(1, 3 * P, K)
+        add_mask(0, 0, K, not_cb_all[:, 0, :], score_0)
+        add_mask(1, 2 * P, 3 * P, not_cb_1[:, 1, 0], score_1b)
+        add_mask(1, 3 * P, K, not_cb_1[:, 1, 1], score_1c)
         row_max(0)
         row_max(1)
         exponential(0)
         exponential(1)
-        def normalise_and_store(b, c0, c1):
+        nc.vector.reciprocal(inv_sum[:, 0:1], row_sum[:, 0:1])
+        nc.vector.tensor_scalar(
+            out=prob[:, 0, :], in0=expd[:, 0, :], scalar1=inv_sum[:, 0:1], scalar2=None, op0=ALU.mult
+        )
+        nc.sync.dma_start(out=out[0], in_=prob[:, 0, :])
+        nc.vector.reciprocal(inv_sum[:, 1:2], row_sum[:, 1:2])
+        for g in range(2):
+            cols = slice(g * 2 * P, (g + 1) * 2 * P)
             nc.vector.tensor_scalar(
-                out=prob[:, b, c0:c1],
-                in0=expd[:, b, c0:c1],
-                scalar1=inv_sum[:, b : b + 1],
+                out=prob[:, 1, cols].rearrange("p (r e) -> p r e", e=2),
+                in0=expd[:, 1, cols].rearrange("p (e r) -> p r e", e=2),
+                scalar1=inv_sum[:, 1:2],
                 scalar2=None,
                 op0=ALU.mult,
             )
-            nc.sync.dma_start(out=out[b][:, c0:c1], in_=prob[:, b, c0:c1])
-
-        nc.vector.reciprocal(inv_sum[:, 0:1], row_sum[:, 0:1])
-        normalise_and_store(0, 0, K)
-        nc.vector.reciprocal(inv_sum[:, 1:2], row_sum[:, 1:2])
-        normalise_and_store(1, 0, K // 2)
-        normalise_and_store(1, K // 2, K)
+            nc.sync.dma_start(out=out[1][:, cols], in_=prob[:, 1, cols])

@@ -36,7 +36,8 @@ def tile_attention_pa_s_kernel(tc, query, context, query_bit, context_bit, W_in,
         qb_col = keep.tile([P, B], BF16)
         bias_col = keep.tile([P, PACK], BF16)
         w_rows = W_in.rearrange("(p u e) d -> u p e d", u=2, e=2)
-        ctx_rows = context.rearrange("b (g p e) d -> b g p e d", g=2, e=2)
+        ctx_rows_0 = context[0].rearrange("(g p e) d -> g p e d", g=2, e=2)
+        ctx_rows_1 = context[1].rearrange("(g e p) d -> g p e d", g=2, e=2)
         nc.sync.dma_start(out=query_sb[:, 0, :], in_=query[0])
         nc.sync.dma_start(
             out=cb_col[:].rearrange("p c e -> p (c e)"), in_=context_bit.rearrange("b (n c) -> (b n) c", c=2 * PACK)
@@ -45,14 +46,14 @@ def tile_attention_pa_s_kernel(tc, query, context, query_bit, context_bit, W_in,
             nc.sync.dma_start(out=w_sb[:, u], in_=w_rows[u])
         nc.sync.dma_start(out=query_sb[:, 1, :], in_=query[1])
         for g in range(2):
-            nc.sync.dma_start(out=ctx_sb[:, 0, g], in_=ctx_rows[0, g])
+            nc.sync.dma_start(out=ctx_sb[:, 0, g], in_=ctx_rows_0[g])
         nc.sync.dma_start(
             out=bias_col[:].rearrange("p (u e) -> p u e", u=2), in_=b_in.rearrange("(p u e) -> p u e", u=2, e=2)
         )
         with nc.allow_non_contiguous_dma(reason="256 single elements, one to a partition and batch"):
             nc.sync.dma_start(out=qb_col[:], in_=query_bit.rearrange("b i -> i b"))
         for g in range(2):
-            nc.sync.dma_start(out=ctx_sb[:, 1, g], in_=ctx_rows[1, g])
+            nc.sync.dma_start(out=ctx_sb[:, 1, g], in_=ctx_rows_1[g])
 
         ident = keep.tile([P, P], F32)
         make_identity(nc, ident[:])
@@ -176,7 +177,7 @@ def tile_attention_pa_s_kernel(tc, query, context, query_bit, context_bit, W_in,
         )
         neg_qb = keep.tile([P, B], F32)
         nc.gpsimd.tensor_scalar(out=neg_qb[:], in0=qb_col[:], scalar1=NEG, scalar2=0.0, op0=ALU.mult, op1=ALU.add)
-        not_cb_1 = not_cb_all[:, 1].rearrange("p (g r e) -> p g e r", g=2, e=2)
+        not_cb_1 = not_cb_all[:, 1].rearrange("p (g e r) -> p g e r", g=2, e=2)
         mask_1a = keep.tile([P, 2, P], F32)
         nc.scalar.activation(out=mask_1a[:], in_=not_cb_1[:, 0], func=ACT.Copy, scale=neg_qb[:, 1:2])
         move_context_1(0)
@@ -258,8 +259,8 @@ def tile_attention_pa_s_kernel(tc, query, context, query_bit, context_bit, W_in,
         for g in range(2):
             cols = slice(g * 2 * P, (g + 1) * 2 * P)
             nc.vector.tensor_scalar(
-                out=prob[:, 1, cols].rearrange("p (r e) -> p r e", e=2),
-                in0=expd[:, 1, cols].rearrange("p (e r) -> p r e", e=2),
+                out=prob[:, 1, cols],
+                in0=expd[:, 1, cols],
                 scalar1=inv_sum[:, 1:2],
                 scalar2=None,
                 op0=ALU.mult,

@@ -36,8 +36,7 @@ def tile_attention_pa_s_kernel(tc, query, context, query_bit, context_bit, W_in,
         qb_col = keep.tile([P, B], BF16)
         bias_col = keep.tile([P, PACK], BF16)
         w_rows = W_in.rearrange("(p u e) d -> u p e d", u=2, e=2)
-        ctx_rows_0 = context[0].rearrange("(g p e) d -> g p e d", g=2, e=2)
-        ctx_rows_1 = context[1].rearrange("(g e p) d -> g p e d", g=2, e=2)
+        ctx_rows = context.rearrange("b (g e p) d -> b g p e d", g=2, e=2)
         nc.sync.dma_start(out=query_sb[:, 0, :], in_=query[0])
         nc.sync.dma_start(
             out=cb_col[:].rearrange("p c e -> p (c e)"), in_=context_bit.rearrange("b (n c) -> (b n) c", c=2 * PACK)
@@ -46,14 +45,14 @@ def tile_attention_pa_s_kernel(tc, query, context, query_bit, context_bit, W_in,
             nc.sync.dma_start(out=w_sb[:, u], in_=w_rows[u])
         nc.sync.dma_start(out=query_sb[:, 1, :], in_=query[1])
         for g in range(2):
-            nc.sync.dma_start(out=ctx_sb[:, 0, g], in_=ctx_rows_0[g])
+            nc.sync.dma_start(out=ctx_sb[:, 0, g], in_=ctx_rows[0, g])
         nc.sync.dma_start(
             out=bias_col[:].rearrange("p (u e) -> p u e", u=2), in_=b_in.rearrange("(p u e) -> p u e", u=2, e=2)
         )
         with nc.allow_non_contiguous_dma(reason="256 single elements, one to a partition and batch"):
             nc.sync.dma_start(out=qb_col[:], in_=query_bit.rearrange("b i -> i b"))
         for g in range(2):
-            nc.sync.dma_start(out=ctx_sb[:, 1, g], in_=ctx_rows_1[g])
+            nc.sync.dma_start(out=ctx_sb[:, 1, g], in_=ctx_rows[1, g])
 
         ident = keep.tile([P, P], F32)
         make_identity(nc, ident[:])
@@ -67,10 +66,9 @@ def tile_attention_pa_s_kernel(tc, query, context, query_bit, context_bit, W_in,
         w_grp = keep.tile([P, 2, 2, P, PACK], BF16, align_bytes=64)
         w_codes = keep.tile([P, 2, 2, P], U32, align_bytes=64)
         w_scales = keep.tile([P, 2, 2, P], U8, align_bytes=64)
-        ctx0_grp = keep.tile([P, 2, P, 2, PACK], BF16, align_bytes=64)
-        ctx1_grp = keep.tile([P, 2, 2, P, PACK], BF16, align_bytes=64)
-        ctx_codes = keep.tile([P, B, 2, 2 * P], U32, align_bytes=64)
-        ctx_scales = keep.tile([P, B, 2, 2 * P], U8, align_bytes=64)
+        ctx_grp = keep.tile([P, B, K, PACK], BF16, align_bytes=64)
+        ctx_codes = keep.tile([P, B, K], U32, align_bytes=64)
+        ctx_scales = keep.tile([P, B, K], U8, align_bytes=64)
         qt_grp = keep.tile([P, B, Q, PACK], BF16, align_bytes=64)
         qt_codes = keep.tile([P, B, Q], U32, align_bytes=64)
         qt_scales = keep.tile([P, B, Q], U8, align_bytes=64)
@@ -101,32 +99,23 @@ def tile_attention_pa_s_kernel(tc, query, context, query_bit, context_bit, W_in,
                 w_scales[:, u].rearrange("p e m -> p (e m)"),
             )
 
-        def quantise_context_0(g):
-            quantise(ctx0_grp[:, g].rearrange("p r e t -> p (r e t)"), ctx_codes[:, 0, g, :], ctx_scales[:, 0, g, :])
-
-        def quantise_context_1(g, e0, e1):
-            cols = slice(e0 * P, e1 * P)
-            quantise(
-                ctx1_grp[:, g, e0:e1].rearrange("p e r t -> p (e r t)"), ctx_codes[:, 1, g, cols], ctx_scales[:, 1, g, cols]
-            )
+        def quantise_context(b, j0, j1):
+            quantise(ctx_grp[:, b, j0:j1].rearrange("p j t -> p (j t)"), ctx_codes[:, b, j0:j1], ctx_scales[:, b, j0:j1])
 
         def quantise_qt(b):
             quantise(qt_grp[:, b].rearrange("p i t -> p (i t)"), qt_codes[:, b, :], qt_scales[:, b, :])
 
-        def move_w(u):
+        def move_w(u, copy):
             bank = transpose_two_row_tiles(w_sb[:].bitcast(F32)[:, u])
-            nc.scalar.copy(out=w_grp[:, u].bitcast(F32), in_=bank[:].rearrange("p e u m -> p e m u"))
+            copy(out=w_grp[:, u].bitcast(F32), in_=bank[:].rearrange("p e u m -> p e m u"))
 
-        def move_context_0(g):
-            bank = transpose_two_row_tiles(ctx_sb[:].bitcast(F32)[:, 0, g])
-            nc.scalar.copy(out=ctx0_grp[:, g].bitcast(F32), in_=bank[:].rearrange("p e u r -> p r e u"))
-
-        def move_context_1(g):
+        def move_context(b, g):
             for e in range(2):
                 bank = psum.tile([P, 2, P], F32, tag="bank")
                 for u in range(2):
-                    nc.tensor.transpose(bank[:, u, :], ctx_sb[:].bitcast(F32)[:, 1, g, e, u : 2 * P : 2], ident[:])
-                nc.scalar.copy(out=ctx1_grp[:, g, e].bitcast(F32), in_=bank[:].rearrange("p u r -> p r u"))
+                    nc.tensor.transpose(bank[:, u, :], ctx_sb[:].bitcast(F32)[:, b, g, e, u : 2 * P : 2], ident[:])
+                j0 = (2 * g + e) * P
+                nc.scalar.copy(out=ctx_grp[:, b, j0 : j0 + P].bitcast(F32), in_=bank[:].rearrange("p u r -> p r u"))
 
         def project(b):
             qt_ps = psum.tile([P, PACK, Q], F32, tag="bank")
@@ -157,36 +146,35 @@ def tile_attention_pa_s_kernel(tc, query, context, query_bit, context_bit, W_in,
         spread_ps = psum.tile([P, PACK, P], F32, tag="bank")
         for c in range(PACK):
             nc.tensor.transpose(spread_ps[:, c, :], not_cb[:].bitcast(F32)[:, c, :].to_broadcast([P, P]), ident[:])
-        move_w(0)
-        quantise_query(0)
-        move_w(1)
-        quantise_w(0)
-        move_query(1)
-        quantise_w(1)
-        move_context_0(0)
-        quantise_query(1)
-        move_context_0(1)
-        quantise_context_0(0)
-        qt_ps0 = project(0)
-        qt_ps1 = project(1)
-        add_bias(0, qt_ps0)
         not_cb_all = keep.tile([P, B, K], BF16)
         nc.scalar.copy(
             out=not_cb_all[:].bitcast(F32).rearrange("p b (n c) -> p b n c", c=PACK),
             in_=spread_ps[:].rearrange("p c (b n) -> p b n c", b=B),
         )
+        move_w(0, nc.vector.tensor_copy)
+        quantise_query(0)
+        move_w(1, nc.scalar.copy)
+        move_query(1)
+        quantise_w(0)
+        quantise_w(1)
+        quantise_query(1)
+        move_context(0, 0)
+        quantise_context(0, 0, 2 * P)
+        move_context(0, 1)
+        quantise_context(0, 2 * P, K)
+        qt_ps0 = project(0)
+        qt_ps1 = project(1)
+        add_bias(0, qt_ps0)
+        add_bias(1, qt_ps1)
         neg_qb = keep.tile([P, B], F32)
         nc.gpsimd.tensor_scalar(out=neg_qb[:], in0=qb_col[:], scalar1=NEG, scalar2=0.0, op0=ALU.mult, op1=ALU.add)
-        not_cb_1 = not_cb_all[:, 1].rearrange("p (g e r) -> p g e r", g=2, e=2)
-        mask_1a = keep.tile([P, 2, P], F32)
-        nc.scalar.activation(out=mask_1a[:], in_=not_cb_1[:, 0], func=ACT.Copy, scale=neg_qb[:, 1:2])
-        move_context_1(0)
-        add_bias(1, qt_ps1)
-        move_context_1(1)
+        mask_1a = keep.tile([P, 2 * P], F32)
+        nc.scalar.activation(out=mask_1a[:], in_=not_cb_all[:, 1, 0 : 2 * P], func=ACT.Copy, scale=neg_qb[:, 1:2])
+        move_context(1, 0)
+        move_context(1, 1)
         quantise_qt(0)
-        quantise_context_0(1)
         quantise_qt(1)
-        quantise_context_1(0, 0, 2)
+        quantise_context(1, 0, 2 * P)
 
         masked = keep.tile([P, B, K], F32)
         expd = keep.tile([P, B, K], F32)
@@ -200,17 +188,17 @@ def tile_attention_pa_s_kernel(tc, query, context, query_bit, context_bit, W_in,
                 out=score_ps[:],
                 lhsT=qt_codes[:, b, :].bitcast(FP8X4),
                 lhsT_scale=qt_scales[:, b, :],
-                rhs=ctx_codes[:, b].rearrange("p g n -> p (g n)")[:, c0:c1].bitcast(FP8X4),
-                rhs_scale=ctx_scales[:, b].rearrange("p g n -> p (g n)")[:, c0:c1],
+                rhs=ctx_codes[:, b, c0:c1].bitcast(FP8X4),
+                rhs_scale=ctx_scales[:, b, c0:c1],
                 start=True,
                 stop=True,
             )
             return score_ps
 
-        def add_mask(b, c0, c1, mask_bits, score_ps):
+        def add_mask(b, c0, c1, score_ps):
             nc.vector.scalar_tensor_tensor(
                 out=masked[:, b, c0:c1],
-                in0=mask_bits,
+                in0=not_cb_all[:, b, c0:c1],
                 scalar=neg_qb[:, b : b + 1],
                 in1=score_ps[:],
                 op0=ALU.mult,
@@ -237,15 +225,15 @@ def tile_attention_pa_s_kernel(tc, query, context, query_bit, context_bit, W_in,
         score_1a = score(1, 0, 2 * P)
         nc.scalar.copy(out=score_1a_sb[:], in_=score_1a[:])
         nc.gpsimd.tensor_tensor(
-            out=masked[:, 1, 0 : 2 * P], in0=score_1a_sb[:], in1=mask_1a[:].rearrange("p e r -> p (e r)"), op=ALU.add
+            out=masked[:, 1, 0 : 2 * P], in0=score_1a_sb[:], in1=mask_1a[:], op=ALU.add
         )
-        quantise_context_1(1, 0, 1)
-        quantise_context_1(1, 1, 2)
+        quantise_context(1, 2 * P, 3 * P)
+        quantise_context(1, 3 * P, K)
         score_1b = score(1, 2 * P, 3 * P)
         score_1c = score(1, 3 * P, K)
-        add_mask(0, 0, K, not_cb_all[:, 0, :], score_0)
-        add_mask(1, 2 * P, 3 * P, not_cb_1[:, 1, 0], score_1b)
-        add_mask(1, 3 * P, K, not_cb_1[:, 1, 1], score_1c)
+        add_mask(0, 0, K, score_0)
+        add_mask(1, 2 * P, 3 * P, score_1b)
+        add_mask(1, 3 * P, K, score_1c)
         row_max(0)
         row_max(1)
         exponential(0)

@@ -49,10 +49,10 @@ def tile_attention_pa_s_kernel(tc, query, context, query_bit, context_bit, W_in,
         nc.sync.dma_start(
             out=bias_col[:].rearrange("p (u e) -> p u e", u=2), in_=b_in.rearrange("(p u e) -> p u e", u=2, e=2)
         )
-        with nc.allow_non_contiguous_dma(reason="256 single elements, one to a partition and batch"):
-            nc.sync.dma_start(out=qb_col[:], in_=query_bit.rearrange("b i -> i b"))
         for g in range(2):
             nc.sync.dma_start(out=ctx_sb[:, 1, g], in_=ctx_rows[1, g])
+        with nc.allow_non_contiguous_dma(reason="256 single elements, one to a partition and batch"):
+            nc.sync.dma_start(out=qb_col[:], in_=query_bit.rearrange("b i -> i b"))
 
         ident = keep.tile([P, P], F32)
         make_identity(nc, ident[:])
@@ -168,10 +168,10 @@ def tile_attention_pa_s_kernel(tc, query, context, query_bit, context_bit, W_in,
         add_bias(1, qt_ps1)
         neg_qb = keep.tile([P, B], F32)
         nc.gpsimd.tensor_scalar(out=neg_qb[:], in0=qb_col[:], scalar1=NEG, scalar2=0.0, op0=ALU.mult, op1=ALU.add)
-        mask_1a = keep.tile([P, 2 * P], F32)
-        nc.scalar.activation(out=mask_1a[:], in_=not_cb_all[:, 1, 0 : 2 * P], func=ACT.Copy, scale=neg_qb[:, 1:2])
         move_context(1, 0)
         move_context(1, 1)
+        mask_1a = keep.tile([P, 2 * P], F32)
+        nc.scalar.activation(out=mask_1a[:], in_=not_cb_all[:, 1, 0 : 2 * P], func=ACT.Copy, scale=neg_qb[:, 1:2])
         quantise_qt(0)
         quantise_qt(1)
         quantise_context(1, 0, 2 * P)

@@ -174,7 +174,8 @@ def tile_attention_pa_s_kernel(tc, query, context, query_bit, context_bit, W_in,
         nc.scalar.activation(out=mask_1a[:], in_=not_cb_all[:, 1, 0 : 2 * P], func=ACT.Copy, scale=neg_qb[:, 1:2])
         quantise_qt(0)
         quantise_qt(1)
-        quantise_context(1, 0, 2 * P)
+        quantise_context(1, 0, P)
+        quantise_context(1, P, 2 * P)
 
         masked = keep.tile([P, B, K], F32)
         expd = keep.tile([P, B, K], F32)
@@ -222,11 +223,11 @@ def tile_attention_pa_s_kernel(tc, query, context, query_bit, context_bit, W_in,
 
         score_1a_sb = keep.tile([P, 2 * P], F32)
         score_0 = score(0, 0, K)
-        score_1a = score(1, 0, 2 * P)
-        nc.scalar.copy(out=score_1a_sb[:], in_=score_1a[:])
-        nc.gpsimd.tensor_tensor(
-            out=masked[:, 1, 0 : 2 * P], in0=score_1a_sb[:], in1=mask_1a[:], op=ALU.add
-        )
+        for c0 in (0, P):
+            cols = slice(c0, c0 + P)
+            score_1a = score(1, c0, c0 + P)
+            nc.scalar.copy(out=score_1a_sb[:, cols], in_=score_1a[:])
+            nc.gpsimd.tensor_tensor(out=masked[:, 1, cols], in0=score_1a_sb[:, cols], in1=mask_1a[:, cols], op=ALU.add)
         quantise_context(1, 2 * P, 3 * P)
         quantise_context(1, 3 * P, K)
         score_1b = score(1, 2 * P, 3 * P)
@@ -238,19 +239,11 @@ def tile_attention_pa_s_kernel(tc, query, context, query_bit, context_bit, W_in,
         row_max(1)
         exponential(0)
         exponential(1)
-        nc.vector.reciprocal(inv_sum[:, 0:1], row_sum[:, 0:1])
-        nc.vector.tensor_scalar(
-            out=prob[:, 0, :], in0=expd[:, 0, :], scalar1=inv_sum[:, 0:1], scalar2=None, op0=ALU.mult
-        )
-        nc.sync.dma_start(out=out[0], in_=prob[:, 0, :])
-        nc.vector.reciprocal(inv_sum[:, 1:2], row_sum[:, 1:2])
-        for g in range(2):
-            cols = slice(g * 2 * P, (g + 1) * 2 * P)
-            nc.vector.tensor_scalar(
-                out=prob[:, 1, cols],
-                in0=expd[:, 1, cols],
-                scalar1=inv_sum[:, 1:2],
-                scalar2=None,
-                op0=ALU.mult,
-            )
-            nc.sync.dma_start(out=out[1][:, cols], in_=prob[:, 1, cols])
+        for b in range(B):
+            nc.vector.reciprocal(inv_sum[:, b : b + 1], row_sum[:, b : b + 1])
+            for c0 in (0, 2 * P):
+                cols = slice(c0, c0 + 2 * P)
+                nc.vector.tensor_scalar(
+                    out=prob[:, b, cols], in0=expd[:, b, cols], scalar1=inv_sum[:, b : b + 1], scalar2=None, op0=ALU.mult
+                )
+                nc.sync.dma_start(out=out[b][:, cols], in_=prob[:, b, cols])

@@ -161,7 +161,6 @@ def tile_attention_pa_s_kernel(tc, query, context, query_bit, context_bit, W_in,
         move_context(0, 0)
         quantise_context(0, 0, 2 * P)
         move_context(0, 1)
-        quantise_context(0, 2 * P, K)
         qt_ps0 = project(0)
         qt_ps1 = project(1)
         add_bias(0, qt_ps0)
@@ -172,6 +171,7 @@ def tile_attention_pa_s_kernel(tc, query, context, query_bit, context_bit, W_in,
         move_context(1, 1)
         mask_1a = keep.tile([P, 2 * P], F32)
         nc.scalar.activation(out=mask_1a[:], in_=not_cb_all[:, 1, 0 : 2 * P], func=ACT.Copy, scale=neg_qb[:, 1:2])
+        quantise_context(0, 2 * P, K)
         quantise_qt(0)
         quantise_qt(1)
         quantise_context(1, 0, P)

@@ -151,8 +151,8 @@ def tile_attention_pa_s_kernel(tc, query, context, query_bit, context_bit, W_in,
             out=not_cb_all[:].bitcast(F32).rearrange("p b (n c) -> p b n c", c=PACK),
             in_=spread_ps[:].rearrange("p c (b n) -> p b n c", b=B),
         )
-        move_w(0, nc.vector.tensor_copy)
         quantise_query(0)
+        move_w(0, nc.vector.tensor_copy)
         move_w(1, nc.scalar.copy)
         move_query(1)
         quantise_w(0)
@@ -161,6 +161,7 @@ def tile_attention_pa_s_kernel(tc, query, context, query_bit, context_bit, W_in,
         move_context(0, 0)
         quantise_context(0, 0, 2 * P)
         move_context(0, 1)
+        quantise_context(0, 2 * P, 3 * P)
         qt_ps0 = project(0)
         qt_ps1 = project(1)
         add_bias(0, qt_ps0)
@@ -171,7 +172,7 @@ def tile_attention_pa_s_kernel(tc, query, context, query_bit, context_bit, W_in,
         move_context(1, 1)
         mask_1a = keep.tile([P, 2 * P], F32)
         nc.scalar.activation(out=mask_1a[:], in_=not_cb_all[:, 1, 0 : 2 * P], func=ACT.Copy, scale=neg_qb[:, 1:2])
-        quantise_context(0, 2 * P, K)
+        quantise_context(0, 3 * P, K)
         quantise_qt(0)
         quantise_qt(1)
         quantise_context(1, 0, P)

from contextlib import ExitStack

import concourse.mybir as mybir
from concourse.masks import make_identity

F32 = mybir.dt.float32
BF16 = mybir.dt.bfloat16
U32 = mybir.dt.uint32
U8 = mybir.dt.uint8
FP8X4 = mybir.dt.float8_e4m3fn_x4
ALU = mybir.AluOpType
ACT = mybir.ActivationFunctionType

P = 128
B = 2
Q = 128
K = 512
D = 512
PACK = 4
NEG = -10000.0

FLOPS = 2 * B * Q * D * D + 2 * B * Q * K * D


def tile_attention_pa_s_kernel(tc, query, context, query_bit, context_bit, W_in, b_in, out):
    nc = tc.nc
    with ExitStack() as ctx:
        keep = ctx.enter_context(tc.tile_pool(name="keep", bufs=1))
        psum = ctx.enter_context(tc.psum_pool(name="psum", bufs=8))
        ctx.enter_context(tc.manual_schedule())

        query_sb = keep.tile([P, B, D], BF16)
        w_sb = keep.tile([P, 2, 2, D], BF16)
        ctx_sb = keep.tile([P, B, 2, 2, D], BF16)
        cb_col = keep.tile([P, PACK, 2], BF16)
        qb_col = keep.tile([P, B], BF16)
        bias_col = keep.tile([P, PACK], BF16)
        w_rows = W_in.rearrange("(p u e) d -> u p e d", u=2, e=2)
        ctx_rows = context.rearrange("b (g e p) d -> b g p e d", g=2, e=2)
        nc.sync.dma_start(out=query_sb[:, 0, :], in_=query[0])
        nc.sync.dma_start(
            out=cb_col[:].rearrange("p c e -> p (c e)"), in_=context_bit.rearrange("b (n c) -> (b n) c", c=2 * PACK)
        )
        for u in range(2):
            nc.sync.dma_start(out=w_sb[:, u], in_=w_rows[u])
        nc.sync.dma_start(out=query_sb[:, 1, :], in_=query[1])
        for g in range(2):
            nc.sync.dma_start(out=ctx_sb[:, 0, g], in_=ctx_rows[0, g])
        nc.sync.dma_start(
            out=bias_col[:].rearrange("p (u e) -> p u e", u=2), in_=b_in.rearrange("(p u e) -> p u e", u=2, e=2)
        )
        for g in range(2):
            nc.sync.dma_start(out=ctx_sb[:, 1, g], in_=ctx_rows[1, g])
        with nc.allow_non_contiguous_dma(reason="256 single elements, one to a partition and batch"):
            nc.sync.dma_start(out=qb_col[:], in_=query_bit.rearrange("b i -> i b"))

        ident = keep.tile([P, P], F32)
        make_identity(nc, ident[:])
        warm = keep.tile([P, 1], F32)
        nc.vector.memset(warm[:], 0.0)
        nc.scalar.activation(out=warm[:], in_=warm[:], func=ACT.Exp)

        query_grp = keep.tile([P, B, Q, PACK], BF16, align_bytes=64)
        query_codes = keep.tile([P, B, Q], U32, align_bytes=64)
        query_scales = keep.tile([P, B, Q], U8, align_bytes=64)
        w_grp = keep.tile([P, 2, 2, P, PACK], BF16, align_bytes=64)
        w_codes = keep.tile([P, 2, 2, P], U32, align_bytes=64)
        w_scales = keep.tile([P, 2, 2, P], U8, align_bytes=64)
        ctx_grp = keep.tile([P, B, K, PACK], BF16, align_bytes=64)
        ctx_codes = keep.tile([P, B, K], U32, align_bytes=64)
        ctx_scales = keep.tile([P, B, K], U8, align_bytes=64)
        qt_grp = keep.tile([P, B, Q, PACK], BF16, align_bytes=64)
        qt_codes = keep.tile([P, B, Q], U32, align_bytes=64)
        qt_scales = keep.tile([P, B, Q], U8, align_bytes=64)

        def transpose_two_row_tiles(words):
            bank = psum.tile([P, 2, 2, P], F32, tag="bank")
            for a in range(2):
                for u in range(2):
                    nc.tensor.transpose(bank[:, a, u, :], words[:, a, u : 2 * P : 2], ident[:])
            return bank

        def quantise(grp, codes, scales):
            nc.vector.quantize_mx(out=codes.bitcast(FP8X4), scales=scales, in_=grp)

        def quantise_query(b):
            quantise(query_grp[:, b].rearrange("p i t -> p (i t)"), query_codes[:, b, :], query_scales[:, b, :])

        def move_query(b):
            bank = psum.tile([P, 2, P], F32, tag="bank")
            for u in range(2):
                nc.tensor.transpose(bank[:, u, :], query_sb[:].bitcast(F32)[:, b, u : 2 * P : 2], ident[:])
            nc.vector.tensor_copy(out=query_grp[:, b].bitcast(F32), in_=bank[:].rearrange("p u i -> p i u"))

        def quantise_w(u):
            quantise(
                w_grp[:, u].rearrange("p e m t -> p (e m t)"),
                w_codes[:, u].rearrange("p e m -> p (e m)"),
                w_scales[:, u].rearrange("p e m -> p (e m)"),
            )

        def quantise_context(b, j0, j1):
            quantise(ctx_grp[:, b, j0:j1].rearrange("p j t -> p (j t)"), ctx_codes[:, b, j0:j1], ctx_scales[:, b, j0:j1])

        def quantise_qt(b):
            quantise(qt_grp[:, b].rearrange("p i t -> p (i t)"), qt_codes[:, b, :], qt_scales[:, b, :])

        def move_w(u, copy):
            bank = transpose_two_row_tiles(w_sb[:].bitcast(F32)[:, u])
            copy(out=w_grp[:, u].bitcast(F32), in_=bank[:].rearrange("p e u m -> p e m u"))

        def move_context(b, g):
            for e in range(2):
                bank = psum.tile([P, 2, P], F32, tag="bank")
                for u in range(2):
                    nc.tensor.transpose(bank[:, u, :], ctx_sb[:].bitcast(F32)[:, b, g, e, u : 2 * P : 2], ident[:])
                j0 = (2 * g + e) * P
                nc.scalar.copy(out=ctx_grp[:, b, j0 : j0 + P].bitcast(F32), in_=bank[:].rearrange("p u r -> p r u"))

        def project(b):
            qt_ps = psum.tile([P, PACK, Q], F32, tag="bank")
            for u in range(2):
                for e in range(2):
                    nc.tensor.matmul_mx(
                        out=qt_ps[:, 2 * u + e, :],
                        lhsT=w_codes[:, u, e, :].bitcast(FP8X4),
                        lhsT_scale=w_scales[:, u, e, :],
                        rhs=query_codes[:, b, :].bitcast(FP8X4),
                        rhs_scale=query_scales[:, b, :],
                        start=True,
                        stop=True,
                    )
            return qt_ps

        def add_bias(b, qt_ps):
            nc.vector.tensor_tensor(
                out=qt_grp[:, b],
                in0=qt_ps[:].rearrange("p t i -> p i t"),
                in1=bias_col[:].unsqueeze(1).to_broadcast([P, Q, PACK]),
                op=ALU.add,
            )

        not_cb = keep.tile([P, PACK, 2], BF16)
        nc.vector.tensor_scalar(out=not_cb[:], in0=cb_col[:], scalar1=-1.0, scalar2=1.0, op0=ALU.mult, op1=ALU.add)
        move_query(0)
        spread_ps = psum.tile([P, PACK, P], F32, tag="bank")
        for c in range(PACK):
            nc.tensor.transpose(spread_ps[:, c, :], not_cb[:].bitcast(F32)[:, c, :].to_broadcast([P, P]), ident[:])
        not_cb_all = keep.tile([P, B, K], BF16)
        nc.scalar.copy(
            out=not_cb_all[:].bitcast(F32).rearrange("p b (n c) -> p b n c", c=PACK),
            in_=spread_ps[:].rearrange("p c (b n) -> p b n c", b=B),
        )
        quantise_query(0)
        move_w(0, nc.vector.tensor_copy)
        move_w(1, nc.scalar.copy)
        move_query(1)
        quantise_w(0)
        quantise_w(1)
        quantise_query(1)
        move_context(0, 0)
        quantise_context(0, 0, 2 * P)
        move_context(0, 1)
        quantise_context(0, 2 * P, 3 * P)
        qt_ps0 = project(0)
        qt_ps1 = project(1)
        add_bias(0, qt_ps0)
        add_bias(1, qt_ps1)
        neg_qb = keep.tile([P, B], F32)
        nc.gpsimd.tensor_scalar(out=neg_qb[:], in0=qb_col[:], scalar1=NEG, scalar2=0.0, op0=ALU.mult, op1=ALU.add)
        move_context(1, 0)
        move_context(1, 1)
        mask_1a = keep.tile([P, 2 * P], F32)
        nc.scalar.activation(out=mask_1a[:], in_=not_cb_all[:, 1, 0 : 2 * P], func=ACT.Copy, scale=neg_qb[:, 1:2])
        quantise_context(0, 3 * P, K)
        quantise_qt(0)
        quantise_qt(1)
        quantise_context(1, 0, P)
        quantise_context(1, P, 2 * P)

        masked = keep.tile([P, B, K], F32)
        expd = keep.tile([P, B, K], F32)
        prob = keep.tile([P, B, K], F32)
        neg_max = keep.tile([P, B], F32)
        row_sum = keep.tile([P, B], F32)
        inv_sum = keep.tile([P, B], F32)
        def score(b, c0, c1):
            score_ps = psum.tile([P, c1 - c0], F32, tag="bank")
            nc.tensor.matmul_mx(
                out=score_ps[:],
                lhsT=qt_codes[:, b, :].bitcast(FP8X4),
                lhsT_scale=qt_scales[:, b, :],
                rhs=ctx_codes[:, b, c0:c1].bitcast(FP8X4),
                rhs_scale=ctx_scales[:, b, c0:c1],
                start=True,
                stop=True,
            )
            return score_ps

        def add_mask(b, c0, c1, score_ps):
            nc.vector.scalar_tensor_tensor(
                out=masked[:, b, c0:c1],
                in0=not_cb_all[:, b, c0:c1],
                scalar=neg_qb[:, b : b + 1],
                in1=score_ps[:],
                op0=ALU.mult,
                op1=ALU.add,
            )

        def row_max(b):
            nc.vector.tensor_reduce(
                out=neg_max[:, b : b + 1], in_=masked[:, b, :], axis=mybir.AxisListType.X, op=ALU.max, negate=True
            )

        def exponential(b):
            nc.scalar.activation(
                out=expd[:, b, :],
                in_=masked[:, b, :],
                func=ACT.Exp,
                bias=neg_max[:, b : b + 1],
                scale=1.0,
                accum_out=row_sum[:, b : b + 1],
            )

        score_1a_sb = keep.tile([P, 2 * P], F32)
        score_0 = score(0, 0, K)
        for c0 in (0, P):
            cols = slice(c0, c0 + P)
            score_1a = score(1, c0, c0 + P)
            nc.scalar.copy(out=score_1a_sb[:, cols], in_=score_1a[:])
            nc.gpsimd.tensor_tensor(out=masked[:, 1, cols], in0=score_1a_sb[:, cols], in1=mask_1a[:, cols], op=ALU.add)
        quantise_context(1, 2 * P, 3 * P)
        quantise_context(1, 3 * P, K)
        score_1b = score(1, 2 * P, 3 * P)
        score_1c = score(1, 3 * P, K)
        add_mask(0, 0, K, score_0)
        add_mask(1, 2 * P, 3 * P, score_1b)
        add_mask(1, 3 * P, K, score_1c)
        row_max(0)
        row_max(1)
        exponential(0)
        exponential(1)
        for b in range(B):
            nc.vector.reciprocal(inv_sum[:, b : b + 1], row_sum[:, b : b + 1])
            for c0 in (0, 2 * P):
                cols = slice(c0, c0 + 2 * P)
                nc.vector.tensor_scalar(
                    out=prob[:, b, cols], in0=expd[:, b, cols], scalar1=inv_sum[:, b : b + 1], scalar2=None, op0=ALU.mult
                )
                nc.sync.dma_start(out=out[b][:, cols], in_=prob[:, b, cols])
